import numpy as np
import ml_dtypes


def mxq(x, axis, fmt="e4m3"):
    dtype, down = {"e4m3": (ml_dtypes.float8_e4m3fn, 7), "e5m2": (ml_dtypes.float8_e5m2, 14)}[fmt]
    v = np.moveaxis(np.asarray(x, np.float32).astype(ml_dtypes.bfloat16).astype(np.float64), axis, -1)
    blocks = v.reshape(v.shape[:-1] + (-1, 32))
    amax = np.abs(blocks).max(-1, keepdims=True)
    byte = np.maximum(np.where(amax > 0, np.frexp(amax)[1] - 1 + 127, 0) - down, 1)
    scale = np.exp2(byte - 127.0)
    codes = (blocks / scale).astype(np.float32).astype(dtype).astype(np.float64)
    return np.moveaxis((codes * scale).reshape(v.shape), -1, axis)


WIDE = False


def mx_kscale(k):
    if not WIDE:
        return np.ones(k)
    levels = np.array([10, -10, 5, -5, 0])
    if k % 512:
        return np.exp2(np.random.permutation(np.resize(levels, k // 32))).repeat(32)
    a = np.empty((k // 512, 16))
    for p in range(k // 512):
        a[p, :8] = np.random.permutation(np.resize(levels, 8))
        for g in range(8):
            far = levels[np.abs(levels - a[p, g]) >= 10]
            a[p, g + 8] = far[np.random.randint(len(far))]
    return np.exp2(a.ravel()).repeat(32)


BF16 = ml_dtypes.bfloat16


def bf(x):
    return np.asarray(x, np.float32).astype(BF16)


def f64(x):
    return np.asarray(x).astype(np.float64)


B, S, IN, OUT, SP = 4, 32, 4096, 4096, 640


def setup_inputs():
    s = mx_kscale(IN)
    return {"x": bf(np.random.standard_normal((B, S, IN)) * s),
            "weights": bf(np.random.standard_normal((OUT, IN)) / np.sqrt(IN) / s[None, :])}


def reference(x, weights):
    x = f64(x)
    weights = f64(weights)
    size_out = x.shape[:-1] + (OUT,)
    xf = x.reshape(-1, x.shape[-1])
    xq = mxq(xf, 1, "e4m3")
    w_sparse = weights[:SP, :]
    w_dense = weights[SP:, :]
    out_sparse = xq @ mxq(w_sparse, 1, "e4m3").T
    out_dense = xq @ mxq(w_dense, 1, "e4m3").T
    out = np.concatenate([out_sparse, out_dense], axis=1)
    return out.reshape(size_out)

@@ -1,0 +1,171 @@
+from contextlib import ExitStack
+
+import concourse.mybir as mybir
+from concourse.masks import make_identity
+
+BF16 = mybir.dt.bfloat16
+F32 = mybir.dt.float32
+U32 = mybir.dt.uint32
+U8 = mybir.dt.uint8
+FP8X4 = mybir.dt.float8_e4m3fn_x4
+
+P = 128
+K = 4096
+OUT = 4096
+PASSES = K // 512
+CHUNKS = OUT // P
+LAST = CHUNKS - 1
+AHEAD = 12
+RUN = 1
+LATE_FROM = 3
+FLOPS = 2 * P * K * OUT
+
+
+def tile_myinterleavedmodule_kernel(tc, x, weights, out):
+    nc = tc.nc
+    xf = x.flatten_outer_dims()
+    of = out.flatten_outer_dims()
+    with ExitStack() as ctx:
+        const = ctx.enter_context(tc.tile_pool(name="const", bufs=1))
+        raw = ctx.enter_context(tc.tile_pool(name="raw", bufs=AHEAD))
+        grp = ctx.enter_context(tc.tile_pool(name="grp", bufs=3))
+        qnt = ctx.enter_context(tc.tile_pool(name="qnt", bufs=5))
+        tps = ctx.enter_context(tc.psum_pool(name="tps", bufs=6))
+        aps = ctx.enter_context(tc.psum_pool(name="aps", bufs=2))
+        ctx.enter_context(tc.manual_schedule())
+
+        ident = const.tile([P, P], F32, name="ident")
+        make_identity(nc, ident[:])
+        o_sb = const.tile([P, OUT], F32, name="o_sb")
+
+        def load(rows, pool, name, pieces):
+            t = pool.tile([P, K], BF16, name=name)
+            w = K // pieces
+            for i in range(pieces):
+                nc.sync.dma_start(out=t[:, i * w : (i + 1) * w], in_=rows[:, i * w : (i + 1) * w])
+            return t
+
+        def load_chunk(c):
+            pieces = 4 if c in (0, LAST) else 1
+            return load(weights[c * P : (c + 1) * P, :], raw, "w_sb", pieces)
+
+        def transposes(t, g0, ng):
+            words = t[:].bitcast(F32)
+            bank = tps.tile([P, 2 * ng, P], F32, name="bank")
+            for j in range(2 * ng):
+                w0 = 2 * (g0 + j // 2) * P
+                every_2nd = slice(w0 + j % 2, w0 + 2 * P, 2)
+                nc.tensor.transpose(bank[:, j, :], words[:, every_2nd], ident[:])
+            return bank
+
+        def regroup(copy, bank, grouped, g0, ng):
+            dst = grouped[:].bitcast(F32).rearrange("p (g r u) -> p g r u", g=PASSES, u=2)
+            copy(out=dst[:, g0 : g0 + ng, :, :], in_=bank[:].rearrange("p (g u) r -> p g r u", u=2))
+
+        def quantise(grouped, codes, scales, g0, ng):
+            c0 = g0 * P
+            c1 = c0 + ng * P
+            nc.vector.quantize_mx(
+                out=codes[:, c0:c1].bitcast(FP8X4),
+                scales=scales[:, c0:c1],
+                in_=grouped[:, 4 * c0 : 4 * c1],
+            )
+
+        x_sb = load(xf, const, "x_sb", 4)
+        w_sb = {}
+        for c in range(AHEAD):
+            w_sb[c] = load_chunk(c)
+
+        x_banks = [transposes(x_sb, 2 * b, 2) for b in range(4)]
+        x_grouped = grp.tile([P, K], BF16, name="grouped", align_bytes=64)
+        x_codes = const.tile([P, PASSES * P], U32, name="x_codes", align_bytes=64)
+        x_scales = const.tile([P, PASSES * P], U8, name="x_scales", align_bytes=64)
+        regroup(nc.scalar.copy, x_banks[0], x_grouped, 0, 2)
+        regroup(nc.vector.tensor_copy, x_banks[1], x_grouped, 2, 2)
+        regroup(nc.scalar.copy, x_banks[2], x_grouped, 4, 2)
+        regroup(nc.vector.tensor_copy, x_banks[3], x_grouped, 6, 2)
+        quantise(x_grouped, x_codes, x_scales, 0, 4)
+        quantise(x_grouped, x_codes, x_scales, 4, 4)
+
+        w_q = {}
+        acc = {}
+        late = []
+
+        def multiply(m):
+            if m % 4 == 0 or m == LAST:
+                acc[m] = aps.tile([P, 512], F32, name="acc")
+                dst = acc[m][:, 0:P]
+            else:
+                dst = acc[m - m % 4][:, (m % 4) * P : (m % 4 + 1) * P]
+            codes, scales = w_q[m]
+            for g in range(PASSES):
+                s = slice(g * P, (g + 1) * P)
+                nc.tensor.matmul_mx(
+                    out=dst,
+                    lhsT=x_codes[:, s].bitcast(FP8X4),
+                    lhsT_scale=x_scales[:, s],
+                    rhs=codes[:, s].bitcast(FP8X4),
+                    rhs_scale=scales[:, s],
+                    start=(g == 0),
+                    stop=(g == PASSES - 1),
+                )
+
+        def finish(first, count):
+            cols = slice(first * P, (first + count) * P)
+            nc.scalar.copy(out=o_sb[:, cols], in_=acc[first][:, 0 : count * P])
+            if first // 4 < LATE_FROM:
+                nc.scalar.dma_start(out=of[:, cols], in_=o_sb[:, cols])
+            else:
+                late.append(cols)
+
+        loaded = AHEAD
+        multiplied = 0
+        sent = 0
+        for c in range(CHUNKS):
+            if c < LAST:
+                banks = [transposes(w_sb[c], 2 * b, 2) for b in range(4)]
+            else:
+                banks = [transposes(w_sb[c], 2 * b, 2) for b in range(3)]
+                banks.append(transposes(w_sb[c], 6, 1))
+                banks.append(transposes(w_sb[c], 7, 1))
+            if loaded < CHUNKS:
+                w_sb[loaded] = load_chunk(loaded)
+                loaded += 1
+            done = list(range(multiplied, c)) if (c % RUN == 0 or c == LAST) else []
+            for m in done:
+                multiply(m)
+            multiplied += len(done)
+            grouped = grp.tile([P, K], BF16, name="grouped", align_bytes=64)
+            codes = qnt.tile([P, PASSES * P], U32, name="codes", align_bytes=64)
+            scales = qnt.tile([P, PASSES * P], U8, name="scales", align_bytes=64)
+            w_q[c] = (codes, scales)
+            if c < LAST:
+                regroup(nc.scalar.copy, banks[0], grouped, 0, 2)
+                regroup(nc.scalar.copy, banks[1], grouped, 2, 2)
+                regroup(nc.scalar.copy, banks[2], grouped, 4, 2)
+                regroup(nc.vector.tensor_copy, banks[3], grouped, 6, 2)
+                quantise(grouped, codes, scales, 0, 4)
+                quantise(grouped, codes, scales, 4, 4)
+            else:
+                regroup(nc.scalar.copy, banks[0], grouped, 0, 2)
+                regroup(nc.vector.tensor_copy, banks[1], grouped, 2, 2)
+                regroup(nc.scalar.copy, banks[2], grouped, 4, 2)
+                quantise(grouped, codes, scales, 0, 2)
+                quantise(grouped, codes, scales, 2, 2)
+                regroup(nc.scalar.copy, banks[3], grouped, 6, 1)
+                regroup(nc.vector.tensor_copy, banks[4], grouped, 7, 1)
+                quantise(grouped, codes, scales, 4, 2)
+                quantise(grouped, codes, scales, 6, 2)
+            for m in done:
+                if m % 4 == 3:
+                    finish(m - 3, 4)
+                elif m == LAST - 1:
+                    finish(m - 2, 3)
+            if loaded == CHUNKS:
+                for cols in late[sent:]:
+                    nc.sync.dma_start(out=of[:, cols], in_=o_sb[:, cols])
+                sent = len(late)
+        multiply(LAST)
+        finish(LAST, 1)
+        for cols in late[sent:]:
+            nc.sync.dma_start(out=of[:, cols], in_=o_sb[:, cols])

@@ -17,6 +17,7 @@ CHUNKS = OUT // P
 LAST = CHUNKS - 1
 AHEAD = 12
 RUN = 1
+EARLY = 4
 LATE_FROM = 3
 FLOPS = 2 * P * K * OUT
 
@@ -30,6 +31,7 @@ def tile_myinterleavedmodule_kernel(tc, x, weights, out):
         raw = ctx.enter_context(tc.tile_pool(name="raw", bufs=AHEAD))
         grp = ctx.enter_context(tc.tile_pool(name="grp", bufs=3))
         qnt = ctx.enter_context(tc.tile_pool(name="qnt", bufs=5))
+        prm = ctx.enter_context(tc.tile_pool(name="prm", bufs=4))
         tps = ctx.enter_context(tc.psum_pool(name="tps", bufs=6))
         aps = ctx.enter_context(tc.psum_pool(name="aps", bufs=2))
         ctx.enter_context(tc.manual_schedule())
@@ -49,13 +51,23 @@ def tile_myinterleavedmodule_kernel(tc, x, weights, out):
             pieces = 4 if c in (0, LAST) else 1
             return load(weights[c * P : (c + 1) * P, :], raw, "w_sb", pieces)
 
-        def transposes(t, g0, ng):
+        def permute(t):
+            n = EARLY * 2 * P
+            perm = prm.tile([P, 2, n // 16, 8], F32, name="perm")
+            src = t[:].bitcast(F32)[:, 0:n].rearrange("p (b u e) -> p u b e", u=2, e=8)
+            nc.vector.tensor_copy(out=perm[:], in_=src)
+            return perm
+
+        def transposes(t, g0, ng, perm=None):
             words = t[:].bitcast(F32)
             bank = tps.tile([P, 2 * ng, P], F32, name="bank")
             for j in range(2 * ng):
-                w0 = 2 * (g0 + j // 2) * P
-                every_2nd = slice(w0 + j % 2, w0 + 2 * P, 2)
-                nc.tensor.transpose(bank[:, j, :], words[:, every_2nd], ident[:])
+                g = g0 + j // 2
+                if perm is not None and g < EARLY:
+                    stationary = perm[:, j % 2, 16 * g : 16 * (g + 1), :].rearrange("p b e -> p (b e)")
+                else:
+                    stationary = words[:, 2 * g * P + j % 2 : 2 * (g + 1) * P : 2]
+                nc.tensor.transpose(bank[:, j, :], stationary, ident[:])
             return bank
 
         def regroup(copy, bank, grouped, g0, ng):
@@ -76,7 +88,8 @@ def tile_myinterleavedmodule_kernel(tc, x, weights, out):
         for c in range(AHEAD):
             w_sb[c] = load_chunk(c)
 
-        x_banks = [transposes(x_sb, 2 * b, 2) for b in range(4)]
+        x_perm = permute(x_sb)
+        x_banks = [transposes(x_sb, 2 * b, 2, x_perm) for b in range(4)]
         x_grouped = grp.tile([P, K], BF16, name="grouped", align_bytes=64)
         x_codes = const.tile([P, PASSES * P], U32, name="x_codes", align_bytes=64)
         x_scales = const.tile([P, PASSES * P], U8, name="x_scales", align_bytes=64)
@@ -87,6 +100,7 @@ def tile_myinterleavedmodule_kernel(tc, x, weights, out):
         quantise(x_grouped, x_codes, x_scales, 0, 4)
         quantise(x_grouped, x_codes, x_scales, 4, 4)
 
+        w_perm = {c: permute(w_sb[c]) for c in range(2)}
         w_q = {}
         acc = {}
         late = []
@@ -123,9 +137,9 @@ def tile_myinterleavedmodule_kernel(tc, x, weights, out):
         sent = 0
         for c in range(CHUNKS):
             if c < LAST:
-                banks = [transposes(w_sb[c], 2 * b, 2) for b in range(4)]
+                banks = [transposes(w_sb[c], 2 * b, 2, w_perm[c]) for b in range(4)]
             else:
-                banks = [transposes(w_sb[c], 2 * b, 2) for b in range(3)]
+                banks = [transposes(w_sb[c], 2 * b, 2, w_perm[c]) for b in range(3)]
                 banks.append(transposes(w_sb[c], 6, 1))
                 banks.append(transposes(w_sb[c], 7, 1))
             if loaded < CHUNKS:
@@ -144,6 +158,8 @@ def tile_myinterleavedmodule_kernel(tc, x, weights, out):
                 regroup(nc.scalar.copy, banks[1], grouped, 2, 2)
                 regroup(nc.scalar.copy, banks[2], grouped, 4, 2)
                 regroup(nc.vector.tensor_copy, banks[3], grouped, 6, 2)
+                if c + 2 < CHUNKS:
+                    w_perm[c + 2] = permute(w_sb[c + 2])
                 quantise(grouped, codes, scales, 0, 4)
                 quantise(grouped, codes, scales, 4, 4)
             else:

@@ -12,13 +12,18 @@ FP8X4 = mybir.dt.float8_e4m3fn_x4
 P = 128
 K = 4096
 OUT = 4096
-PASSES = K // 512
-CHUNKS = OUT // P
-LAST = CHUNKS - 1
-AHEAD = 12
-RUN = 1
-EARLY = 4
-LATE_FROM = 3
+PASS_K = 512
+PASSES = K // PASS_K
+PASS_WORDS = PASS_K // 2
+ROWS = 4
+GROUP = ROWS * P
+GROUPS = OUT // GROUP
+PERMUTED = 6
+AHEAD = 7
+FIRST_ORDER = ((6,), (7,), (0, 1), (2, 3, 4, 5))
+ORDER = ((6, 0, 1, 2), (7, 3, 4, 5))
+LAST_ORDER = ((0, 1, 2, 3), (4, 5), (6,), (7,))
+VECTOR_BANKS = (3, 7)
 FLOPS = 2 * P * K * OUT
 
 
@@ -29,9 +34,9 @@ def tile_myinterleavedmodule_kernel(tc, x, weights, out):
     with ExitStack() as ctx:
         const = ctx.enter_context(tc.tile_pool(name="const", bufs=1))
         raw = ctx.enter_context(tc.tile_pool(name="raw", bufs=AHEAD))
-        grp = ctx.enter_context(tc.tile_pool(name="grp", bufs=3))
-        qnt = ctx.enter_context(tc.tile_pool(name="qnt", bufs=5))
-        prm = ctx.enter_context(tc.tile_pool(name="prm", bufs=4))
+        prm = ctx.enter_context(tc.tile_pool(name="prm", bufs=6))
+        grp = ctx.enter_context(tc.tile_pool(name="grp", bufs=4))
+        qnt = ctx.enter_context(tc.tile_pool(name="qnt", bufs=9))
         tps = ctx.enter_context(tc.psum_pool(name="tps", bufs=6))
         aps = ctx.enter_context(tc.psum_pool(name="aps", bufs=2))
         ctx.enter_context(tc.manual_schedule())
@@ -40,148 +45,195 @@ def tile_myinterleavedmodule_kernel(tc, x, weights, out):
         make_identity(nc, ident[:])
         o_sb = const.tile([P, OUT], F32, name="o_sb")
 
-        def load(rows, pool, name, pieces):
-            t = pool.tile([P, K], BF16, name=name)
-            w = K // pieces
-            for i in range(pieces):
-                nc.sync.dma_start(out=t[:, i * w : (i + 1) * w], in_=rows[:, i * w : (i + 1) * w])
-            return t
+        def words_of(t):
+            return t.bitcast(F32)
 
-        def load_chunk(c):
-            pieces = 4 if c in (0, LAST) else 1
-            return load(weights[c * P : (c + 1) * P, :], raw, "w_sb", pieces)
+        def permute(dst, row, g0, ng):
+            b0 = 16 * g0
+            b1 = b0 + 16 * ng
+            src = words_of(row)[:, g0 * PASS_WORDS : (g0 + ng) * PASS_WORDS]
+            nc.vector.tensor_copy(out=dst[:, :, b0:b1, :], in_=src.rearrange("p (b u e) -> p u b e", u=2, e=8))
 
-        def permute(t):
-            n = EARLY * 2 * P
-            perm = prm.tile([P, 2, n // 16, 8], F32, name="perm")
-            src = t[:].bitcast(F32)[:, 0:n].rearrange("p (b u e) -> p u b e", u=2, e=8)
-            nc.vector.tensor_copy(out=perm[:], in_=src)
-            return perm
+        def new_perm(pool, name):
+            return pool.tile([P, 2, 16 * PERMUTED, 8], F32, name=name)
 
-        def transposes(t, g0, ng, perm=None):
-            words = t[:].bitcast(F32)
-            bank = tps.tile([P, 2 * ng, P], F32, name="bank")
-            for j in range(2 * ng):
-                g = g0 + j // 2
-                if perm is not None and g < EARLY:
-                    stationary = perm[:, j % 2, 16 * g : 16 * (g + 1), :].rearrange("p b e -> p (b e)")
-                else:
-                    stationary = words[:, 2 * g * P + j % 2 : 2 * (g + 1) * P : 2]
-                nc.tensor.transpose(bank[:, j, :], stationary, ident[:])
+        def stationary(row, perm, g, u):
+            if g < PERMUTED:
+                return perm[:, u, 16 * g : 16 * (g + 1), :].rearrange("p b e -> p (b e)")
+            return words_of(row)[:, g * PASS_WORDS + u : (g + 1) * PASS_WORDS : 2]
+
+        x_sb = const.tile([P, K], BF16, name="x_sb")
+
+        def load_x(g0, ng):
+            cols = slice(g0 * PASS_K, (g0 + ng) * PASS_K)
+            nc.sync.dma_start(out=x_sb[:, cols], in_=xf[:, cols])
+
+        pairs = {}
+
+        def new_pair(G, h):
+            pairs[(G, h)] = raw.tile([P, 2, K], BF16, name="w_sb")
+
+        def load_slice(G, h, g0, ng):
+            rows = weights[G * GROUP : (G + 1) * GROUP, g0 * PASS_K : (g0 + ng) * PASS_K]
+            view = rows.rearrange("(p j) k -> p j k", j=ROWS)
+            cols = slice(g0 * PASS_K, (g0 + ng) * PASS_K)
+            nc.sync.dma_start(out=pairs[(G, h)][:, :, cols], in_=view[:, 2 * h : 2 * h + 2, :])
+
+        def load_pair(G, h):
+            new_pair(G, h)
+            if G == GROUPS - 1:
+                if h == 1:
+                    for step in LAST_ORDER:
+                        for hh in (0, 1):
+                            load_slice(G, hh, step[0], len(step))
+            else:
+                load_slice(G, h, 0, PASSES)
+
+        load_x(6, 2)
+        load_x(0, 6)
+        for h in (0, 1):
+            new_pair(0, h)
+        for step in FIRST_ORDER:
+            for h in (0, 1):
+                load_slice(0, h, step[0], len(step))
+        order = [(G, h) for G in range(1, GROUPS) for h in (0, 1)]
+        loaded = 0
+        for G, h in order[: AHEAD - 2]:
+            load_pair(G, h)
+            loaded += 1
+
+        x_perm = new_perm(const, "x_perm")
+        permute(x_perm, x_sb[:], 0, PERMUTED)
+        x_grouped = const.tile([P, K], BF16, name="x_grouped", align_bytes=64)
+        x_codes = const.tile([P, PASSES * P], U32, name="x_codes", align_bytes=64)
+        x_scales = const.tile([P, PASSES * P], U8, name="x_scales", align_bytes=64)
+
+        def x_bank(g0):
+            bank = tps.tile([P, 4, P], F32, name="bank")
+            for i in range(4):
+                nc.tensor.transpose(bank[:, i, :], stationary(x_sb[:], x_perm, g0 + i // 2, i % 2), ident[:])
             return bank
 
-        def regroup(copy, bank, grouped, g0, ng):
-            dst = grouped[:].bitcast(F32).rearrange("p (g r u) -> p g r u", g=PASSES, u=2)
-            copy(out=dst[:, g0 : g0 + ng, :, :], in_=bank[:].rearrange("p (g u) r -> p g r u", u=2))
+        def x_regroup(copy, bank, g0):
+            dst = words_of(x_grouped[:]).rearrange("p (g r u) -> p g r u", g=PASSES, u=2)
+            copy(out=dst[:, g0 : g0 + 2, :, :], in_=bank[:].rearrange("p (g u) r -> p g r u", u=2))
 
-        def quantise(grouped, codes, scales, g0, ng):
+        def x_quantise(g0, ng):
             c0 = g0 * P
             c1 = c0 + ng * P
             nc.vector.quantize_mx(
-                out=codes[:, c0:c1].bitcast(FP8X4),
-                scales=scales[:, c0:c1],
-                in_=grouped[:, 4 * c0 : 4 * c1],
+                out=x_codes[:, c0:c1].bitcast(FP8X4), scales=x_scales[:, c0:c1], in_=x_grouped[:, 4 * c0 : 4 * c1]
             )
 
-        x_sb = load(xf, const, "x_sb", 4)
-        w_sb = {}
-        for c in range(AHEAD):
-            w_sb[c] = load_chunk(c)
+        x_banks = {g: x_bank(g) for g in (6, 0, 2, 4)}
+        x_regroup(nc.scalar.copy, x_banks[6], 6)
+        x_regroup(nc.vector.tensor_copy, x_banks[0], 0)
+        x_regroup(nc.scalar.copy, x_banks[2], 2)
+        x_regroup(nc.vector.tensor_copy, x_banks[4], 4)
+        x_quantise(0, 4)
+        x_quantise(4, 4)
 
-        x_perm = permute(x_sb)
-        x_banks = [transposes(x_sb, 2 * b, 2, x_perm) for b in range(4)]
-        x_grouped = grp.tile([P, K], BF16, name="grouped", align_bytes=64)
-        x_codes = const.tile([P, PASSES * P], U32, name="x_codes", align_bytes=64)
-        x_scales = const.tile([P, PASSES * P], U8, name="x_scales", align_bytes=64)
-        regroup(nc.scalar.copy, x_banks[0], x_grouped, 0, 2)
-        regroup(nc.vector.tensor_copy, x_banks[1], x_grouped, 2, 2)
-        regroup(nc.scalar.copy, x_banks[2], x_grouped, 4, 2)
-        regroup(nc.vector.tensor_copy, x_banks[3], x_grouped, 6, 2)
-        quantise(x_grouped, x_codes, x_scales, 0, 4)
-        quantise(x_grouped, x_codes, x_scales, 4, 4)
+        perms = {}
 
-        w_perm = {c: permute(w_sb[c]) for c in range(2)}
+        def permute_rows(G, j, g0, ng):
+            if (G, j) not in perms:
+                perms[(G, j)] = new_perm(prm, "w_perm")
+            permute(perms[(G, j)], pairs[(G, j // 2)][:, j % 2, :], g0, ng)
+
+        def transposes(G, g, h):
+            bank = tps.tile([P, 4, P], F32, name="bank")
+            for i in range(4):
+                j = 2 * h + i // 2
+                row = pairs[(G, h)][:, i // 2, :]
+                nc.tensor.transpose(bank[:, i, :], stationary(row, perms.get((G, j)), g, i % 2), ident[:])
+            return bank
+
+        def regroup(copy, bank, grouped, h):
+            dst = words_of(grouped[:]).rearrange("p (j r u) -> p j r u", j=ROWS, u=2)
+            copy(out=dst[:, 2 * h : 2 * h + 2, :, :], in_=bank[:].rearrange("p (j u) r -> p j r u", u=2))
+
         w_q = {}
+
+        def quantise(G, g, grouped):
+            codes = qnt.tile([P, GROUP], U32, name="codes", align_bytes=64)
+            scales = qnt.tile([P, GROUP], U8, name="scales", align_bytes=64)
+            w_q[(G, g)] = (codes, scales)
+            nc.vector.quantize_mx(out=codes[:].bitcast(FP8X4), scales=scales[:], in_=grouped[:])
+
         acc = {}
-        late = []
 
-        def multiply(m):
-            if m % 4 == 0 or m == LAST:
-                acc[m] = aps.tile([P, 512], F32, name="acc")
-                dst = acc[m][:, 0:P]
-            else:
-                dst = acc[m - m % 4][:, (m % 4) * P : (m % 4 + 1) * P]
-            codes, scales = w_q[m]
-            for g in range(PASSES):
-                s = slice(g * P, (g + 1) * P)
-                nc.tensor.matmul_mx(
-                    out=dst,
-                    lhsT=x_codes[:, s].bitcast(FP8X4),
-                    lhsT_scale=x_scales[:, s],
-                    rhs=codes[:, s].bitcast(FP8X4),
-                    rhs_scale=scales[:, s],
-                    start=(g == 0),
-                    stop=(g == PASSES - 1),
-                )
+        def multiply(G, g, first, last):
+            if first:
+                acc[G] = aps.tile([P, GROUP], F32, name="acc")
+            codes, scales = w_q[(G, g)]
+            s = slice(g * P, (g + 1) * P)
+            nc.tensor.matmul_mx(
+                out=acc[G][:],
+                lhsT=x_codes[:, s].bitcast(FP8X4),
+                lhsT_scale=x_scales[:, s],
+                rhs=codes[:].bitcast(FP8X4),
+                rhs_scale=scales[:],
+                start=first,
+                stop=last,
+            )
 
-        def finish(first, count):
-            cols = slice(first * P, (first + count) * P)
-            nc.scalar.copy(out=o_sb[:, cols], in_=acc[first][:, 0 : count * P])
-            if first // 4 < LATE_FROM:
-                nc.scalar.dma_start(out=of[:, cols], in_=o_sb[:, cols])
-            else:
-                late.append(cols)
+        def finish(G):
+            dst = o_sb[:, G * GROUP : (G + 1) * GROUP].rearrange("m (p j) -> m p j", j=ROWS)
+            nc.scalar.copy(out=dst, in_=acc[G][:].rearrange("m (j p) -> m p j", j=ROWS))
 
-        loaded = AHEAD
-        multiplied = 0
-        sent = 0
-        for c in range(CHUNKS):
-            if c < LAST:
-                banks = [transposes(w_sb[c], 2 * b, 2, w_perm[c]) for b in range(4)]
-            else:
-                banks = [transposes(w_sb[c], 2 * b, 2, w_perm[c]) for b in range(3)]
-                banks.append(transposes(w_sb[c], 6, 1))
-                banks.append(transposes(w_sb[c], 7, 1))
-            if loaded < CHUNKS:
-                w_sb[loaded] = load_chunk(loaded)
-                loaded += 1
-            done = list(range(multiplied, c)) if (c % RUN == 0 or c == LAST) else []
-            for m in done:
-                multiply(m)
-            multiplied += len(done)
-            grouped = grp.tile([P, K], BF16, name="grouped", align_bytes=64)
-            codes = qnt.tile([P, PASSES * P], U32, name="codes", align_bytes=64)
-            scales = qnt.tile([P, PASSES * P], U8, name="scales", align_bytes=64)
-            w_q[c] = (codes, scales)
-            if c < LAST:
-                regroup(nc.scalar.copy, banks[0], grouped, 0, 2)
-                regroup(nc.scalar.copy, banks[1], grouped, 2, 2)
-                regroup(nc.scalar.copy, banks[2], grouped, 4, 2)
-                regroup(nc.vector.tensor_copy, banks[3], grouped, 6, 2)
-                if c + 2 < CHUNKS:
-                    w_perm[c + 2] = permute(w_sb[c + 2])
-                quantise(grouped, codes, scales, 0, 4)
-                quantise(grouped, codes, scales, 4, 4)
-            else:
-                regroup(nc.scalar.copy, banks[0], grouped, 0, 2)
-                regroup(nc.vector.tensor_copy, banks[1], grouped, 2, 2)
-                regroup(nc.scalar.copy, banks[2], grouped, 4, 2)
-                quantise(grouped, codes, scales, 0, 2)
-                quantise(grouped, codes, scales, 2, 2)
-                regroup(nc.scalar.copy, banks[3], grouped, 6, 1)
-                regroup(nc.vector.tensor_copy, banks[4], grouped, 7, 1)
-                quantise(grouped, codes, scales, 4, 2)
-                quantise(grouped, codes, scales, 6, 2)
-            for m in done:
-                if m % 4 == 3:
-                    finish(m - 3, 4)
-                elif m == LAST - 1:
-                    finish(m - 2, 3)
-            if loaded == CHUNKS:
-                for cols in late[sent:]:
-                    nc.sync.dma_start(out=of[:, cols], in_=o_sb[:, cols])
-                sent = len(late)
-        multiply(LAST)
-        finish(LAST, 1)
-        for cols in late[sent:]:
-            nc.sync.dma_start(out=of[:, cols], in_=o_sb[:, cols])
+        def store(c0, c1):
+            nc.sync.dma_start(out=of[:, c0:c1], in_=o_sb[:, c0:c1])
+
+        blocks = []
+        for G in range(GROUPS):
+            steps = FIRST_ORDER if G == 0 else LAST_ORDER if G == GROUPS - 1 else ORDER
+            flat = [g for step in steps for g in step]
+            for step in steps:
+                blocks.append([(G, g, flat.index(g)) for g in step])
+
+        pending = []
+        for n, block in enumerate(blocks):
+            banks = {(G, g, h): transposes(G, g, h) for G, g, i in block for h in (0, 1)}
+            for G, g, i in block:
+                if i == PASSES - 1:
+                    for more in order[loaded : loaded + 2]:
+                        load_pair(more[0], more[1])
+                        loaded += 1
+                while pending:
+                    args = pending.pop()
+                    quantise(args[0], args[1], args[2])
+                if G == 0 and i == 1:
+                    for j in range(ROWS):
+                        permute_rows(0, j, 0, 2)
+                if G == 0 and i in (2, 3):
+                    for j in (2 * i - 4, 2 * i - 3):
+                        permute_rows(0, j, 2, 4)
+                if G < GROUPS - 2 and i >= 4:
+                    permute_rows(G + 1, i - 4, 0, PERMUTED)
+                if G == GROUPS - 2 and i >= 4:
+                    permute_rows(G + 1, i - 4, 0, 4)
+                if G == GROUPS - 1 and i in (0, 1):
+                    for j in (2 * i, 2 * i + 1):
+                        permute_rows(G, j, 4, 2)
+                grouped = grp.tile([P, 4 * GROUP], BF16, name="grouped", align_bytes=64)
+                late = G == GROUPS - 1 and i >= 6
+                for h in (0, 1):
+                    on_vector = h == 1 and (i in VECTOR_BANKS or late)
+                    regroup(nc.vector.tensor_copy if on_vector else nc.scalar.copy, banks[(G, g, h)], grouped, h)
+                pending.append((G, g, grouped))
+                if late:
+                    args = pending.pop()
+                    quantise(args[0], args[1], args[2])
+            if n > 0:
+                for G, g, i in blocks[n - 1]:
+                    multiply(G, g, i == 0, i == PASSES - 1)
+                    if i == PASSES - 1:
+                        finish(G)
+            if n == len(blocks) - 4:
+                store(0, (GROUPS - 2) * GROUP)
+            if n == len(blocks) - 3:
+                store((GROUPS - 2) * GROUP, (GROUPS - 1) * GROUP)
+        for G, g, i in blocks[-1]:
+            multiply(G, g, i == 0, i == PASSES - 1)
+        finish(GROUPS - 1)
+        store((GROUPS - 1) * GROUP, OUT)

@@ -14,16 +14,22 @@ K = 4096
 OUT = 4096
 PASS_K = 512
 PASSES = K // PASS_K
-PASS_WORDS = PASS_K // 2
-ROWS = 4
+PAIRS = PASSES // 2
+PAIR_K = 2 * PASS_K
+PAIR_WORDS = PAIR_K // 2
+ROWS = 2
 GROUP = ROWS * P
 GROUPS = OUT // GROUP
-PERMUTED = 6
-AHEAD = 7
-FIRST_ORDER = ((6,), (7,), (0, 1), (2, 3, 4, 5))
-ORDER = ((6, 0, 1, 2), (7, 3, 4, 5))
-LAST_ORDER = ((0, 1, 2, 3), (4, 5), (6,), (7,))
-VECTOR_BANKS = (3, 7)
+LAST = GROUPS - 1
+PERMUTED = 5
+AHEAD = 10
+PERM_LEAD = 6
+BANK_LEAD = 5
+MX_LAG = 2
+FINISH_LAG = 5
+RUN = 8
+VECTOR_EVERY = 20
+SLICED = (0, LAST)
 FLOPS = 2 * P * K * OUT
 
 
@@ -34,206 +40,214 @@ def tile_myinterleavedmodule_kernel(tc, x, weights, out):
     with ExitStack() as ctx:
         const = ctx.enter_context(tc.tile_pool(name="const", bufs=1))
         raw = ctx.enter_context(tc.tile_pool(name="raw", bufs=AHEAD))
-        prm = ctx.enter_context(tc.tile_pool(name="prm", bufs=6))
-        grp = ctx.enter_context(tc.tile_pool(name="grp", bufs=4))
-        qnt = ctx.enter_context(tc.tile_pool(name="qnt", bufs=9))
-        tps = ctx.enter_context(tc.psum_pool(name="tps", bufs=6))
-        aps = ctx.enter_context(tc.psum_pool(name="aps", bufs=2))
+        prm = ctx.enter_context(tc.tile_pool(name="prm", bufs=10))
+        grp = ctx.enter_context(tc.tile_pool(name="grp", bufs=8))
+        qnt = ctx.enter_context(tc.tile_pool(name="qnt", bufs=8))
+        tps = ctx.enter_context(tc.psum_pool(name="tps", bufs=BANK_LEAD + 1))
+        aps = ctx.enter_context(tc.psum_pool(name="aps", bufs=7 - BANK_LEAD))
         ctx.enter_context(tc.manual_schedule())
 
         ident = const.tile([P, P], F32, name="ident")
         make_identity(nc, ident[:])
         o_sb = const.tile([P, OUT], F32, name="o_sb")
-
-        def words_of(t):
-            return t.bitcast(F32)
-
-        def permute(dst, row, g0, ng):
-            b0 = 16 * g0
-            b1 = b0 + 16 * ng
-            src = words_of(row)[:, g0 * PASS_WORDS : (g0 + ng) * PASS_WORDS]
-            nc.vector.tensor_copy(out=dst[:, :, b0:b1, :], in_=src.rearrange("p (b u e) -> p u b e", u=2, e=8))
-
-        def new_perm(pool, name):
-            return pool.tile([P, 2, 16 * PERMUTED, 8], F32, name=name)
-
-        def stationary(row, perm, g, u):
-            if g < PERMUTED:
-                return perm[:, u, 16 * g : 16 * (g + 1), :].rearrange("p b e -> p (b e)")
-            return words_of(row)[:, g * PASS_WORDS + u : (g + 1) * PASS_WORDS : 2]
-
         x_sb = const.tile([P, K], BF16, name="x_sb")
-
-        def load_x(g0, ng):
-            cols = slice(g0 * PASS_K, (g0 + ng) * PASS_K)
-            nc.sync.dma_start(out=x_sb[:, cols], in_=xf[:, cols])
-
-        pairs = {}
-
-        def new_pair(G, h):
-            pairs[(G, h)] = raw.tile([P, 2, K], BF16, name="w_sb")
-
-        def load_slice(G, h, g0, ng):
-            rows = weights[G * GROUP : (G + 1) * GROUP, g0 * PASS_K : (g0 + ng) * PASS_K]
-            view = rows.rearrange("(p j) k -> p j k", j=ROWS)
-            cols = slice(g0 * PASS_K, (g0 + ng) * PASS_K)
-            nc.sync.dma_start(out=pairs[(G, h)][:, :, cols], in_=view[:, 2 * h : 2 * h + 2, :])
-
-        def load_pair(G, h):
-            new_pair(G, h)
-            if G == GROUPS - 1:
-                if h == 1:
-                    for step in LAST_ORDER:
-                        for hh in (0, 1):
-                            load_slice(G, hh, step[0], len(step))
-            else:
-                load_slice(G, h, 0, PASSES)
-
-        load_x(6, 2)
-        load_x(0, 6)
-        for h in (0, 1):
-            new_pair(0, h)
-        for step in FIRST_ORDER:
-            for h in (0, 1):
-                load_slice(0, h, step[0], len(step))
-        order = [(G, h) for G in range(1, GROUPS) for h in (0, 1)]
-        loaded = 0
-        for G, h in order[: AHEAD - 2]:
-            load_pair(G, h)
-            loaded += 1
-
-        x_perm = new_perm(const, "x_perm")
-        permute(x_perm, x_sb[:], 0, PERMUTED)
         x_grouped = const.tile([P, K], BF16, name="x_grouped", align_bytes=64)
         x_codes = const.tile([P, PASSES * P], U32, name="x_codes", align_bytes=64)
         x_scales = const.tile([P, PASSES * P], U8, name="x_scales", align_bytes=64)
 
-        def x_bank(g0):
-            bank = tps.tile([P, 4, P], F32, name="bank")
-            for i in range(4):
-                nc.tensor.transpose(bank[:, i, :], stationary(x_sb[:], x_perm, g0 + i // 2, i % 2), ident[:])
-            return bank
+        cells = {}
 
-        def x_regroup(copy, bank, g0):
-            dst = words_of(x_grouped[:]).rearrange("p (g r u) -> p g r u", g=PASSES, u=2)
-            copy(out=dst[:, g0 : g0 + 2, :, :], in_=bank[:].rearrange("p (g u) r -> p g r u", u=2))
+        def load_x(b0, nb):
+            cols = slice(b0 * PAIR_K, (b0 + nb) * PAIR_K)
+            nc.sync.dma_start(out=x_sb[:, cols], in_=xf[:, cols])
+            for b in range(b0, b0 + nb):
+                cells[("x", 0, 0, b)] = (x_sb, b * PAIR_K)
 
-        def x_quantise(g0, ng):
-            c0 = g0 * P
-            c1 = c0 + ng * P
-            nc.vector.quantize_mx(
-                out=x_codes[:, c0:c1].bitcast(FP8X4), scales=x_scales[:, c0:c1], in_=x_grouped[:, 4 * c0 : 4 * c1]
-            )
+        def load_w(G, j0, nj, b0, nb, tile, at):
+            n = nb * PAIR_K
+            dst = tile[:, at : at + nj * n].rearrange("p (j k) -> p j k", k=n)
+            view = weights[G * GROUP : (G + 1) * GROUP, b0 * PAIR_K : b0 * PAIR_K + n]
+            nc.sync.dma_start(out=dst, in_=view.rearrange("(p j) k -> p j k", j=ROWS)[:, j0 : j0 + nj, :])
+            for j in range(nj):
+                for b in range(nb):
+                    cells[("w", G, j0 + j, b0 + b)] = (tile, at + j * n + b * PAIR_K)
 
-        x_banks = {g: x_bank(g) for g in (6, 0, 2, 4)}
-        x_regroup(nc.scalar.copy, x_banks[6], 6)
-        x_regroup(nc.vector.tensor_copy, x_banks[0], 0)
-        x_regroup(nc.scalar.copy, x_banks[2], 2)
-        x_regroup(nc.vector.tensor_copy, x_banks[4], 4)
-        x_quantise(0, 4)
-        x_quantise(4, 4)
+        loads = []
+        halves = []
+        units = []
+        X_UNITS = [("x", 0, 0, b) for b in range(PAIRS)]
+        for G in range(GROUPS):
+            if G in SLICED:
+                for b in (3, 0, 1, 2) if G == 0 else (0, 1, 2, 3):
+                    loads.append((G, b))
+                    units.extend(("w", G, j, b) for j in range(ROWS))
+            else:
+                for j in range(ROWS):
+                    loads.append((G, j))
+                    units.extend(("w", G, j, b) for b in (3, 0, 1, 2))
+        head = []
+        for i, b in enumerate((3, 0, 1, 2)):
+            head.append(X_UNITS[b])
+            head.extend(units[2 * i : 2 * i + 2])
+        units = head + units[8:]
+
+        def load_next():
+            G, what = loads.pop(0)
+            if G in SLICED:
+                if not halves:
+                    tile = raw.tile([P, K], BF16, name="w_sb")
+                    halves.extend([(tile, K // 2), (tile, 0)])
+                tile, at = halves.pop()
+                load_w(G, 0, ROWS, what, 1, tile, at)
+            else:
+                tile = raw.tile([P, K], BF16, name="w_sb")
+                load_w(G, what, 1, 0, PAIRS, tile, 0)
+
+        def words_of(unit):
+            tile, at = cells[unit]
+            return tile[:, at : at + PAIR_K].bitcast(F32)
 
         perms = {}
 
-        def permute_rows(G, j, g0, ng):
-            if (G, j) not in perms:
-                perms[(G, j)] = new_perm(prm, "w_perm")
-            permute(perms[(G, j)], pairs[(G, j // 2)][:, j % 2, :], g0, ng)
+        def permute(unit):
+            n = min(max(PERMUTED - 2 * unit[3], 0), 2)
+            if n > 0:
+                perm = prm.tile([P, 2, 2 * P], F32, name="perm")
+                nc.vector.tensor_copy(
+                    out=perm[:, :, 0 : n * P].rearrange("p u (b e) -> p u b e", e=8),
+                    in_=words_of(unit)[:, 0 : 2 * n * P].rearrange("p (b u e) -> p u b e", u=2, e=8),
+                )
+                perms[unit] = perm
 
-        def transposes(G, g, h):
+        banks = {}
+
+        def transposes(unit):
             bank = tps.tile([P, 4, P], F32, name="bank")
-            for i in range(4):
-                j = 2 * h + i // 2
-                row = pairs[(G, h)][:, i // 2, :]
-                nc.tensor.transpose(bank[:, i, :], stationary(row, perms.get((G, j)), g, i % 2), ident[:])
-            return bank
+            words = words_of(unit)
+            for h in (0, 1):
+                for u in (0, 1):
+                    if 2 * unit[3] + h < PERMUTED:
+                        stationary = perms[unit][:, u, h * P : (h + 1) * P]
+                    else:
+                        stationary = words[:, 2 * h * P + u : 2 * (h + 1) * P : 2]
+                    nc.tensor.transpose(bank[:, 2 * h + u, :], stationary, ident[:])
+            banks[unit] = bank
 
-        def regroup(copy, bank, grouped, h):
-            dst = words_of(grouped[:]).rearrange("p (j r u) -> p j r u", j=ROWS, u=2)
-            copy(out=dst[:, 2 * h : 2 * h + 2, :, :], in_=bank[:].rearrange("p (j u) r -> p j r u", u=2))
+        grouped = {}
+        quants = {}
+        copied = {}
 
-        w_q = {}
+        def regroup(unit, copy):
+            kind, G, j, b = unit
+            src = banks[unit][:].rearrange("p (h u) r -> p h r u", u=2)
+            if kind == "x":
+                dst = x_grouped[:].bitcast(F32).rearrange("p (g r u) -> p g r u", g=PASSES, u=2)
+                copy(out=dst[:, 2 * b : 2 * b + 2, :, :], in_=src)
+            else:
+                if (G, b) not in grouped:
+                    grouped[(G, b)] = grp.tile([P, 2 * GROUP * 4], BF16, name="grouped", align_bytes=64)
+                dst = grouped[(G, b)][:].bitcast(F32).rearrange("p (h j r u) -> p h j r u", h=2, j=ROWS, u=2)
+                copy(out=dst[:, :, j, :, :], in_=src)
+            copied[(kind, G, b)] = copied.get((kind, G, b), 0) + 1
+            return copied[(kind, G, b)] == (1 if kind == "x" else ROWS)
 
-        def quantise(G, g, grouped):
-            codes = qnt.tile([P, GROUP], U32, name="codes", align_bytes=64)
-            scales = qnt.tile([P, GROUP], U8, name="scales", align_bytes=64)
-            w_q[(G, g)] = (codes, scales)
-            nc.vector.quantize_mx(out=codes[:].bitcast(FP8X4), scales=scales[:], in_=grouped[:])
+        def quantise(kind, G, b):
+            if kind == "x":
+                s = slice(2 * b * P, 2 * (b + 1) * P)
+                nc.vector.quantize_mx(
+                    out=x_codes[:, s].bitcast(FP8X4),
+                    scales=x_scales[:, s],
+                    in_=x_grouped[:, 8 * b * P : 8 * (b + 1) * P],
+                )
+            else:
+                codes = qnt.tile([P, 2 * GROUP], U32, name="codes", align_bytes=64)
+                scales = qnt.tile([P, 2 * GROUP], U8, name="scales", align_bytes=64)
+                quants[(G, b)] = (codes, scales)
+                nc.vector.quantize_mx(out=codes[:].bitcast(FP8X4), scales=scales[:], in_=grouped[(G, b)][:])
 
         acc = {}
+        passes_done = {}
 
-        def multiply(G, g, first, last):
-            if first:
-                acc[G] = aps.tile([P, GROUP], F32, name="acc")
-            codes, scales = w_q[(G, g)]
-            s = slice(g * P, (g + 1) * P)
-            nc.tensor.matmul_mx(
-                out=acc[G][:],
-                lhsT=x_codes[:, s].bitcast(FP8X4),
-                lhsT_scale=x_scales[:, s],
-                rhs=codes[:].bitcast(FP8X4),
-                rhs_scale=scales[:],
-                start=first,
-                stop=last,
-            )
+        def multiply(G, b):
+            if G not in acc:
+                bank = aps.tile([P, 2 * GROUP], F32, name="acc")
+                acc[G] = bank[:, 0:GROUP]
+                if G % 2 == 0 and G + 1 < LAST:
+                    acc[G + 1] = bank[:, GROUP : 2 * GROUP]
+                    acc[(G, "both")] = bank
+            codes, scales = quants[(G, b)]
+            for h in (0, 1):
+                s = slice((2 * b + h) * P, (2 * b + h + 1) * P)
+                w = slice(h * GROUP, (h + 1) * GROUP)
+                k = passes_done.get(G, 0)
+                nc.tensor.matmul_mx(
+                    out=acc[G],
+                    lhsT=x_codes[:, s].bitcast(FP8X4),
+                    lhsT_scale=x_scales[:, s],
+                    rhs=codes[:, w].bitcast(FP8X4),
+                    rhs_scale=scales[:, w],
+                    start=(k == 0),
+                    stop=(k == PASSES - 1),
+                )
+                passes_done[G] = k + 1
+            return passes_done[G] == PASSES
+
+        def store(G0, G1):
+            cols = slice(G0 * GROUP, G1 * GROUP)
+            nc.sync.dma_start(out=of[:, cols], in_=o_sb[:, cols])
 
         def finish(G):
-            dst = o_sb[:, G * GROUP : (G + 1) * GROUP].rearrange("m (p j) -> m p j", j=ROWS)
-            nc.scalar.copy(out=dst, in_=acc[G][:].rearrange("m (j p) -> m p j", j=ROWS))
+            if G % 2 == 0 and G + 1 < LAST:
+                return
+            pair = (G - 1, "both") in acc
+            first = G - 1 if pair else G
+            n = 2 if pair else 1
+            src = acc[(first, "both")][:] if pair else acc[G]
+            dst = o_sb[:, first * GROUP : (G + 1) * GROUP].rearrange("m (a p j) -> m a p j", a=n, j=ROWS)
+            nc.scalar.copy(out=dst, in_=src.rearrange("m (a j p) -> m a p j", a=n, j=ROWS))
+            if G == LAST - 2:
+                store(0, LAST - 1)
+            elif G > LAST - 2:
+                store(G, G + 1)
 
-        def store(c0, c1):
-            nc.sync.dma_start(out=of[:, c0:c1], in_=o_sb[:, c0:c1])
+        for b in (3, 0, 1, 2):
+            load_x(b, 1)
+            load_next()
 
-        blocks = []
-        for G in range(GROUPS):
-            steps = FIRST_ORDER if G == 0 else LAST_ORDER if G == GROUPS - 1 else ORDER
-            flat = [g for step in steps for g in step]
-            for step in steps:
-                blocks.append([(G, g, flat.index(g)) for g in step])
-
-        pending = []
-        for n, block in enumerate(blocks):
-            banks = {(G, g, h): transposes(G, g, h) for G, g, i in block for h in (0, 1)}
-            for G, g, i in block:
-                if i == PASSES - 1:
-                    for more in order[loaded : loaded + 2]:
-                        load_pair(more[0], more[1])
-                        loaded += 1
-                while pending:
-                    args = pending.pop()
-                    quantise(args[0], args[1], args[2])
-                if G == 0 and i == 1:
-                    for j in range(ROWS):
-                        permute_rows(0, j, 0, 2)
-                if G == 0 and i in (2, 3):
-                    for j in (2 * i - 4, 2 * i - 3):
-                        permute_rows(0, j, 2, 4)
-                if G < GROUPS - 2 and i >= 4:
-                    permute_rows(G + 1, i - 4, 0, PERMUTED)
-                if G == GROUPS - 2 and i >= 4:
-                    permute_rows(G + 1, i - 4, 0, 4)
-                if G == GROUPS - 1 and i in (0, 1):
-                    for j in (2 * i, 2 * i + 1):
-                        permute_rows(G, j, 4, 2)
-                grouped = grp.tile([P, 4 * GROUP], BF16, name="grouped", align_bytes=64)
-                late = G == GROUPS - 1 and i >= 6
-                for h in (0, 1):
-                    on_vector = h == 1 and (i in VECTOR_BANKS or late)
-                    regroup(nc.vector.tensor_copy if on_vector else nc.scalar.copy, banks[(G, g, h)], grouped, h)
-                pending.append((G, g, grouped))
-                if late:
-                    args = pending.pop()
-                    quantise(args[0], args[1], args[2])
-            if n > 0:
-                for G, g, i in blocks[n - 1]:
-                    multiply(G, g, i == 0, i == PASSES - 1)
-                    if i == PASSES - 1:
-                        finish(G)
-            if n == len(blocks) - 4:
-                store(0, (GROUPS - 2) * GROUP)
-            if n == len(blocks) - 3:
-                store((GROUPS - 2) * GROUP, (GROUPS - 1) * GROUP)
-        for G, g, i in blocks[-1]:
-            multiply(G, g, i == 0, i == PASSES - 1)
-        finish(GROUPS - 1)
-        store((GROUPS - 1) * GROUP, OUT)
+        while len(loads) > 2 * GROUPS + 2 - 10:
+            load_next()
+        n = len(units)
+        waiting = []
+        ready = []
+        closed = []
+        for t in range(-PERM_LEAD, n + 1):
+            if t + PERM_LEAD < n:
+                permute(units[t + PERM_LEAD])
+            if 0 <= t + BANK_LEAD < n:
+                unit = units[t + BANK_LEAD]
+                transposes(unit)
+                if unit[0] == "w" and t + BANK_LEAD >= 11 and (t + BANK_LEAD) % 4 == 3 and loads:
+                    load_next()
+                    if loads and halves:
+                        load_next()
+            if t < 0:
+                continue
+            for q in waiting:
+                quantise(q[0], q[1], q[2])
+                if q[0] == "w":
+                    ready.append((q[1], q[2], t))
+            waiting = []
+            if t < n:
+                unit = units[t]
+                if regroup(unit, nc.vector.tensor_copy if t % VECTOR_EVERY == VECTOR_EVERY - 1 else nc.scalar.copy):
+                    waiting.append((unit[0], unit[2 - 1], unit[3]))
+            if t >= 6 and (t % RUN == 0 or t > n - 6):
+                lag = MX_LAG if t < n - 6 else 0
+                for G, b, made in [r for r in ready if r[2] <= t - lag]:
+                    if multiply(G, b):
+                        closed.append((G, t))
+                ready = [r for r in ready if r[2] > t - lag]
+            for G, at in closed:
+                if at <= t - FINISH_LAG or t == n:
+                    finish(G)
+            closed = [r for r in closed if r[1] > t - FINISH_LAG and t < n]

@@ -27,7 +27,7 @@ PERM_LEAD = 6
 BANK_LEAD = 5
 MX_LAG = 2
 FINISH_LAG = 5
-RUN = 8
+RUN = 4
 VECTOR_EVERY = 20
 SLICED = (0, LAST)
 FLOPS = 2 * P * K * OUT
@@ -67,7 +67,7 @@ def tile_myinterleavedmodule_kernel(tc, x, weights, out):
             n = nb * PAIR_K
             dst = tile[:, at : at + nj * n].rearrange("p (j k) -> p j k", k=n)
             view = weights[G * GROUP : (G + 1) * GROUP, b0 * PAIR_K : b0 * PAIR_K + n]
-            nc.sync.dma_start(out=dst, in_=view.rearrange("(p j) k -> p j k", j=ROWS)[:, j0 : j0 + nj, :])
+            nc.sync.dma_start(out=dst, in_=view.rearrange("(j p) k -> p j k", j=ROWS)[:, j0 : j0 + nj, :])
             for j in range(nj):
                 for b in range(nb):
                     cells[("w", G, j0 + j, b0 + b)] = (tile, at + j * n + b * PAIR_K)
@@ -201,14 +201,12 @@ def tile_myinterleavedmodule_kernel(tc, x, weights, out):
                 return
             pair = (G - 1, "both") in acc
             first = G - 1 if pair else G
-            n = 2 if pair else 1
             src = acc[(first, "both")][:] if pair else acc[G]
-            dst = o_sb[:, first * GROUP : (G + 1) * GROUP].rearrange("m (a p j) -> m a p j", a=n, j=ROWS)
-            nc.scalar.copy(out=dst, in_=src.rearrange("m (a j p) -> m a p j", a=n, j=ROWS))
-            if G == LAST - 2:
-                store(0, LAST - 1)
-            elif G > LAST - 2:
-                store(G, G + 1)
+            nc.scalar.copy(out=o_sb[:, first * GROUP : (G + 1) * GROUP], in_=src)
+            if G == LAST - 4:
+                store(0, G + 1)
+            elif G > LAST - 4:
+                store(first, G + 1)
 
         for b in (3, 0, 1, 2):
             load_x(b, 1)
@@ -232,11 +230,12 @@ def tile_myinterleavedmodule_kernel(tc, x, weights, out):
                         load_next()
             if t < 0:
                 continue
-            for q in waiting:
+            now = len(waiting) if t < 16 or t > n - 20 else 1 if t % 2 == 0 else 0
+            for q in waiting[:now]:
                 quantise(q[0], q[1], q[2])
                 if q[0] == "w":
                     ready.append((q[1], q[2], t))
-            waiting = []
+            waiting = waiting[now:]
             if t < n:
                 unit = units[t]
                 if regroup(unit, nc.vector.tensor_copy if t % VECTOR_EVERY == VECTOR_EVERY - 1 else nc.scalar.copy):

@@ -21,13 +21,13 @@ ROWS = 2
 GROUP = ROWS * P
 GROUPS = OUT // GROUP
 LAST = GROUPS - 1
-PERMUTED = 5
+PERMUTED = 6
 AHEAD = 10
 PERM_LEAD = 6
 BANK_LEAD = 5
 MX_LAG = 2
 FINISH_LAG = 5
-RUN = 4
+RUN = 8
 VECTOR_EVERY = 20
 SLICED = (0, LAST)
 FLOPS = 2 * P * K * OUT
@@ -40,9 +40,9 @@ def tile_myinterleavedmodule_kernel(tc, x, weights, out):
     with ExitStack() as ctx:
         const = ctx.enter_context(tc.tile_pool(name="const", bufs=1))
         raw = ctx.enter_context(tc.tile_pool(name="raw", bufs=AHEAD))
-        prm = ctx.enter_context(tc.tile_pool(name="prm", bufs=10))
+        prm = ctx.enter_context(tc.tile_pool(name="prm", bufs=6))
         grp = ctx.enter_context(tc.tile_pool(name="grp", bufs=8))
-        qnt = ctx.enter_context(tc.tile_pool(name="qnt", bufs=8))
+        qnt = ctx.enter_context(tc.tile_pool(name="qnt", bufs=10))
         tps = ctx.enter_context(tc.psum_pool(name="tps", bufs=BANK_LEAD + 1))
         aps = ctx.enter_context(tc.psum_pool(name="aps", bufs=7 - BANK_LEAD))
         ctx.enter_context(tc.manual_schedule())
@@ -110,14 +110,21 @@ def tile_myinterleavedmodule_kernel(tc, x, weights, out):
         perms = {}
 
         def permute(unit):
-            n = min(max(PERMUTED - 2 * unit[3], 0), 2)
-            if n > 0:
-                perm = prm.tile([P, 2, 2 * P], F32, name="perm")
-                nc.vector.tensor_copy(
-                    out=perm[:, :, 0 : n * P].rearrange("p u (b e) -> p u b e", e=8),
-                    in_=words_of(unit)[:, 0 : 2 * n * P].rearrange("p (b u e) -> p u b e", u=2, e=8),
-                )
-                perms[unit] = perm
+            if 2 * unit[3] >= PERMUTED or unit in perms:
+                return
+            kind, G, j, b = unit
+            whole = kind == "w" and G not in SLICED
+            pairs = (0, 1, 2) if whole else (b,)
+            n = min(PERMUTED - 2 * pairs[0], 2 * len(pairs))
+            perm = prm.tile([P, 2, n * P], F32, name="perm")
+            tile, at = cells[(kind, G, j, pairs[0])]
+            src = tile[:, at : at + n * PASS_K].bitcast(F32)
+            nc.vector.tensor_copy(
+                out=perm[:].rearrange("p u (b e) -> p u b e", e=8),
+                in_=src.rearrange("p (b u e) -> p u b e", u=2, e=8),
+            )
+            for i, b in enumerate(pairs):
+                perms[(kind, G, j, b)] = perm[:, :, 2 * i * P : 2 * (i + 1) * P]
 
         banks = {}
 

@@ -27,7 +27,7 @@ PERM_LEAD = 6
 BANK_LEAD = 5
 MX_LAG = 2
 FINISH_LAG = 5
-RUN = 8
+RUN = 5
 VECTOR_EVERY = 20
 SLICED = (0, LAST)
 FLOPS = 2 * P * K * OUT

from contextlib import ExitStack

import concourse.mybir as mybir
from concourse.masks import make_identity

BF16 = mybir.dt.bfloat16
F32 = mybir.dt.float32
U32 = mybir.dt.uint32
U8 = mybir.dt.uint8
FP8X4 = mybir.dt.float8_e4m3fn_x4

P = 128
K = 4096
OUT = 4096
PASS_K = 512
PASSES = K // PASS_K
PAIRS = PASSES // 2
PAIR_K = 2 * PASS_K
PAIR_WORDS = PAIR_K // 2
ROWS = 2
GROUP = ROWS * P
GROUPS = OUT // GROUP
LAST = GROUPS - 1
PERMUTED = 6
AHEAD = 10
PERM_LEAD = 6
BANK_LEAD = 5
MX_LAG = 2
FINISH_LAG = 5
RUN = 5
VECTOR_EVERY = 20
SLICED = (0, LAST)
FLOPS = 2 * P * K * OUT


def tile_myinterleavedmodule_kernel(tc, x, weights, out):
    nc = tc.nc
    xf = x.flatten_outer_dims()
    of = out.flatten_outer_dims()
    with ExitStack() as ctx:
        const = ctx.enter_context(tc.tile_pool(name="const", bufs=1))
        raw = ctx.enter_context(tc.tile_pool(name="raw", bufs=AHEAD))
        prm = ctx.enter_context(tc.tile_pool(name="prm", bufs=6))
        grp = ctx.enter_context(tc.tile_pool(name="grp", bufs=8))
        qnt = ctx.enter_context(tc.tile_pool(name="qnt", bufs=10))
        tps = ctx.enter_context(tc.psum_pool(name="tps", bufs=BANK_LEAD + 1))
        aps = ctx.enter_context(tc.psum_pool(name="aps", bufs=7 - BANK_LEAD))
        ctx.enter_context(tc.manual_schedule())

        ident = const.tile([P, P], F32, name="ident")
        make_identity(nc, ident[:])
        o_sb = const.tile([P, OUT], F32, name="o_sb")
        x_sb = const.tile([P, K], BF16, name="x_sb")
        x_grouped = const.tile([P, K], BF16, name="x_grouped", align_bytes=64)
        x_codes = const.tile([P, PASSES * P], U32, name="x_codes", align_bytes=64)
        x_scales = const.tile([P, PASSES * P], U8, name="x_scales", align_bytes=64)

        cells = {}

        def load_x(b0, nb):
            cols = slice(b0 * PAIR_K, (b0 + nb) * PAIR_K)
            nc.sync.dma_start(out=x_sb[:, cols], in_=xf[:, cols])
            for b in range(b0, b0 + nb):
                cells[("x", 0, 0, b)] = (x_sb, b * PAIR_K)

        def load_w(G, j0, nj, b0, nb, tile, at):
            n = nb * PAIR_K
            dst = tile[:, at : at + nj * n].rearrange("p (j k) -> p j k", k=n)
            view = weights[G * GROUP : (G + 1) * GROUP, b0 * PAIR_K : b0 * PAIR_K + n]
            nc.sync.dma_start(out=dst, in_=view.rearrange("(j p) k -> p j k", j=ROWS)[:, j0 : j0 + nj, :])
            for j in range(nj):
                for b in range(nb):
                    cells[("w", G, j0 + j, b0 + b)] = (tile, at + j * n + b * PAIR_K)

        loads = []
        halves = []
        units = []
        X_UNITS = [("x", 0, 0, b) for b in range(PAIRS)]
        for G in range(GROUPS):
            if G in SLICED:
                for b in (3, 0, 1, 2) if G == 0 else (0, 1, 2, 3):
                    loads.append((G, b))
                    units.extend(("w", G, j, b) for j in range(ROWS))
            else:
                for j in range(ROWS):
                    loads.append((G, j))
                    units.extend(("w", G, j, b) for b in (3, 0, 1, 2))
        head = []
        for i, b in enumerate((3, 0, 1, 2)):
            head.append(X_UNITS[b])
            head.extend(units[2 * i : 2 * i + 2])
        units = head + units[8:]

        def load_next():
            G, what = loads.pop(0)
            if G in SLICED:
                if not halves:
                    tile = raw.tile([P, K], BF16, name="w_sb")
                    halves.extend([(tile, K // 2), (tile, 0)])
                tile, at = halves.pop()
                load_w(G, 0, ROWS, what, 1, tile, at)
            else:
                tile = raw.tile([P, K], BF16, name="w_sb")
                load_w(G, what, 1, 0, PAIRS, tile, 0)

        def words_of(unit):
            tile, at = cells[unit]
            return tile[:, at : at + PAIR_K].bitcast(F32)

        perms = {}

        def permute(unit):
            if 2 * unit[3] >= PERMUTED or unit in perms:
                return
            kind, G, j, b = unit
            whole = kind == "w" and G not in SLICED
            pairs = (0, 1, 2) if whole else (b,)
            n = min(PERMUTED - 2 * pairs[0], 2 * len(pairs))
            perm = prm.tile([P, 2, n * P], F32, name="perm")
            tile, at = cells[(kind, G, j, pairs[0])]
            src = tile[:, at : at + n * PASS_K].bitcast(F32)
            nc.vector.tensor_copy(
                out=perm[:].rearrange("p u (b e) -> p u b e", e=8),
                in_=src.rearrange("p (b u e) -> p u b e", u=2, e=8),
            )
            for i, b in enumerate(pairs):
                perms[(kind, G, j, b)] = perm[:, :, 2 * i * P : 2 * (i + 1) * P]

        banks = {}

        def transposes(unit):
            bank = tps.tile([P, 4, P], F32, name="bank")
            words = words_of(unit)
            for h in (0, 1):
                for u in (0, 1):
                    if 2 * unit[3] + h < PERMUTED:
                        stationary = perms[unit][:, u, h * P : (h + 1) * P]
                    else:
                        stationary = words[:, 2 * h * P + u : 2 * (h + 1) * P : 2]
                    nc.tensor.transpose(bank[:, 2 * h + u, :], stationary, ident[:])
            banks[unit] = bank

        grouped = {}
        quants = {}
        copied = {}

        def regroup(unit, copy):
            kind, G, j, b = unit
            src = banks[unit][:].rearrange("p (h u) r -> p h r u", u=2)
            if kind == "x":
                dst = x_grouped[:].bitcast(F32).rearrange("p (g r u) -> p g r u", g=PASSES, u=2)
                copy(out=dst[:, 2 * b : 2 * b + 2, :, :], in_=src)
            else:
                if (G, b) not in grouped:
                    grouped[(G, b)] = grp.tile([P, 2 * GROUP * 4], BF16, name="grouped", align_bytes=64)
                dst = grouped[(G, b)][:].bitcast(F32).rearrange("p (h j r u) -> p h j r u", h=2, j=ROWS, u=2)
                copy(out=dst[:, :, j, :, :], in_=src)
            copied[(kind, G, b)] = copied.get((kind, G, b), 0) + 1
            return copied[(kind, G, b)] == (1 if kind == "x" else ROWS)

        def quantise(kind, G, b):
            if kind == "x":
                s = slice(2 * b * P, 2 * (b + 1) * P)
                nc.vector.quantize_mx(
                    out=x_codes[:, s].bitcast(FP8X4),
                    scales=x_scales[:, s],
                    in_=x_grouped[:, 8 * b * P : 8 * (b + 1) * P],
                )
            else:
                codes = qnt.tile([P, 2 * GROUP], U32, name="codes", align_bytes=64)
                scales = qnt.tile([P, 2 * GROUP], U8, name="scales", align_bytes=64)
                quants[(G, b)] = (codes, scales)
                nc.vector.quantize_mx(out=codes[:].bitcast(FP8X4), scales=scales[:], in_=grouped[(G, b)][:])

        acc = {}
        passes_done = {}

        def multiply(G, b):
            if G not in acc:
                bank = aps.tile([P, 2 * GROUP], F32, name="acc")
                acc[G] = bank[:, 0:GROUP]
                if G % 2 == 0 and G + 1 < LAST:
                    acc[G + 1] = bank[:, GROUP : 2 * GROUP]
                    acc[(G, "both")] = bank
            codes, scales = quants[(G, b)]
            for h in (0, 1):
                s = slice((2 * b + h) * P, (2 * b + h + 1) * P)
                w = slice(h * GROUP, (h + 1) * GROUP)
                k = passes_done.get(G, 0)
                nc.tensor.matmul_mx(
                    out=acc[G],
                    lhsT=x_codes[:, s].bitcast(FP8X4),
                    lhsT_scale=x_scales[:, s],
                    rhs=codes[:, w].bitcast(FP8X4),
                    rhs_scale=scales[:, w],
                    start=(k == 0),
                    stop=(k == PASSES - 1),
                )
                passes_done[G] = k + 1
            return passes_done[G] == PASSES

        def store(G0, G1):
            cols = slice(G0 * GROUP, G1 * GROUP)
            nc.sync.dma_start(out=of[:, cols], in_=o_sb[:, cols])

        def finish(G):
            if G % 2 == 0 and G + 1 < LAST:
                return
            pair = (G - 1, "both") in acc
            first = G - 1 if pair else G
            src = acc[(first, "both")][:] if pair else acc[G]
            nc.scalar.copy(out=o_sb[:, first * GROUP : (G + 1) * GROUP], in_=src)
            if G == LAST - 4:
                store(0, G + 1)
            elif G > LAST - 4:
                store(first, G + 1)

        for b in (3, 0, 1, 2):
            load_x(b, 1)
            load_next()

        while len(loads) > 2 * GROUPS + 2 - 10:
            load_next()
        n = len(units)
        waiting = []
        ready = []
        closed = []
        for t in range(-PERM_LEAD, n + 1):
            if t + PERM_LEAD < n:
                permute(units[t + PERM_LEAD])
            if 0 <= t + BANK_LEAD < n:
                unit = units[t + BANK_LEAD]
                transposes(unit)
                if unit[0] == "w" and t + BANK_LEAD >= 11 and (t + BANK_LEAD) % 4 == 3 and loads:
                    load_next()
                    if loads and halves:
                        load_next()
            if t < 0:
                continue
            now = len(waiting) if t < 16 or t > n - 20 else 1 if t % 2 == 0 else 0
            for q in waiting[:now]:
                quantise(q[0], q[1], q[2])
                if q[0] == "w":
                    ready.append((q[1], q[2], t))
            waiting = waiting[now:]
            if t < n:
                unit = units[t]
                if regroup(unit, nc.vector.tensor_copy if t % VECTOR_EVERY == VECTOR_EVERY - 1 else nc.scalar.copy):
                    waiting.append((unit[0], unit[2 - 1], unit[3]))
            if t >= 6 and (t % RUN == 0 or t > n - 6):
                lag = MX_LAG if t < n - 6 else 0
                for G, b, made in [r for r in ready if r[2] <= t - lag]:
                    if multiply(G, b):
                        closed.append((G, t))
                ready = [r for r in ready if r[2] > t - lag]
            for G, at in closed:
                if at <= t - FINISH_LAG or t == n:
                    finish(G)
            closed = [r for r in closed if r[1] > t - FINISH_LAG and t < n]
